import numpy as np
import ml_dtypes


def mxq(x, axis, fmt="e4m3"):
    dtype, down = {"e4m3": (ml_dtypes.float8_e4m3fn, 7), "e5m2": (ml_dtypes.float8_e5m2, 14)}[fmt]
    v = np.moveaxis(np.asarray(x, np.float32).astype(ml_dtypes.bfloat16).astype(np.float64), axis, -1)
    blocks = v.reshape(v.shape[:-1] + (-1, 32))
    amax = np.abs(blocks).max(-1, keepdims=True)
    byte = np.maximum(np.where(amax > 0, np.frexp(amax)[1] - 1 + 127, 0) - down, 1)
    scale = np.exp2(byte - 127.0)
    codes = (blocks / scale).astype(np.float32).astype(dtype).astype(np.float64)
    return np.moveaxis((codes * scale).reshape(v.shape), -1, axis)


WIDE = False


def mx_kscale(k):
    if not WIDE:
        return np.ones(k)
    levels = np.array([10, -10, 5, -5, 0])
    a = np.random.permutation(np.resize(levels, k // 512 * 4)).reshape(k // 512, 4)
    idx = np.arange(k)
    return np.exp2(a[idx // 512, idx % 128 // 32])


BF16 = ml_dtypes.bfloat16


def bf(x):
    return np.asarray(x, np.float32).astype(BF16)


def f64(x):
    return np.asarray(x).astype(np.float64)


N, D, C, M = 3072, 512, 16, 16
LAMDA = 0.00390625
VS = 1.0 / (LAMDA * D)


def setup_inputs():
    s = mx_kscale(D)
    return {"x": bf(np.random.standard_normal((N, D)) * s),
            "x_var": bf(np.random.uniform(0.0, 1.0, (N, D)) * (0.5 + np.random.uniform(0.0, 1.0, (N, 1))) * 2.0 * VS),
            "proto_mean": bf(np.random.standard_normal((C, M, D)) / np.sqrt(D) / s),
            "proto_var": bf(np.random.uniform(0.0, 1.0, (C, M, D)) * (0.5 + np.random.uniform(0.0, 1.0, (C, M, 1))) * 2.0 * VS)}


def reference(x, x_var, proto_mean, proto_var):
    xv, pv = f64(x_var), f64(proto_var)
    dot = (mxq(f64(x), 1, "e4m3") @ mxq(f64(proto_mean), 2, "e4m3").reshape(C * M, D).T).reshape(N, C, M)
    cross = (mxq(np.sqrt(xv), 1, "e4m3") @ mxq(np.sqrt(pv), 2, "e4m3").reshape(C * M, D).T).reshape(N, C, M)
    var_term = xv.sum(-1)[:, None, None] + pv.sum(-1)[None, :, :] - 2.0 * cross
    return -(2.0 - 2.0 * dot + LAMDA * var_term)

@@ -1,0 +1,220 @@
+from contextlib import ExitStack
+
+import concourse.mybir as mybir
+from concourse.masks import make_identity
+
+FP8X4 = mybir.dt.float8_e4m3fn_x4
+BF16 = mybir.dt.bfloat16
+F32 = mybir.dt.float32
+U32 = mybir.dt.uint32
+U8 = mybir.dt.uint8
+ALU = mybir.AluOpType
+ACT = mybir.ActivationFunctionType
+
+P = 128
+N_ROWS = 3072
+D = 512
+J = 256
+LAMDA = 0.00390625
+TILES = N_ROWS // P
+PAIRS = TILES // 2
+
+FLOPS = 2 * 2 * N_ROWS * D * J
+
+
+def tile_probprotoseghead_kernel(tc, x, x_var, proto_mean, proto_var, out):
+    nc = tc.nc
+    x_v = x.rearrange("(p t) d -> p t d", t=TILES)
+    v_v = x_var.rearrange("(p t) d -> p t d", t=TILES)
+    o_v = out.rearrange("(p t) c m -> p t (c m)", t=TILES)
+    pm_v = proto_mean.rearrange("c m d -> (c m) d").rearrange("(h p) d -> p h d", p=P)
+    pv_v = proto_var.rearrange("c m d -> (c m) d").rearrange("(h p) d -> p h d", p=P)
+
+    with ExitStack() as ctx:
+        const = ctx.enter_context(tc.tile_pool(name="const", bufs=1))
+        inp = ctx.enter_context(tc.tile_pool(name="inp", bufs=1))
+        gpool = ctx.enter_context(tc.tile_pool(name="gpool", bufs=3))
+        qpool = ctx.enter_context(tc.tile_pool(name="qpool", bufs=4))
+        opool = ctx.enter_context(tc.tile_pool(name="opool", bufs=4))
+        jpool = ctx.enter_context(tc.tile_pool(name="jpool", bufs=2))
+        ps_x = ctx.enter_context(tc.psum_pool(name="ps_x", bufs=2))
+        ps_v = ctx.enter_context(tc.psum_pool(name="ps_v", bufs=3))
+        ps_o = ctx.enter_context(tc.psum_pool(name="ps_o", bufs=3))
+
+        ident = const.tile([P, P], F32, name="ident")
+        make_identity(nc, ident[:])
+
+        pv_sb = const.tile([P, 2, D], BF16, name="pv_sb")
+        nc.sync.dma_start(out=pv_sb[:], in_=pv_v)
+        pm_sb = const.tile([P, 2, D], BF16, name="pm_sb")
+        nc.sync.dma_start(out=pm_sb[:], in_=pm_v)
+        x_sb = []
+        v_sb = []
+        for i in range(PAIRS):
+            vt_in = inp.tile([P, 2, D], BF16, name="v%d" % i)
+            nc.sync.dma_start(out=vt_in[:], in_=v_v[:, 2 * i : 2 * i + 2, :])
+            xt_in = inp.tile([P, 2, D], BF16, name="x%d" % i)
+            nc.sync.dma_start(out=xt_in[:], in_=x_v[:, 2 * i : 2 * i + 2, :])
+            v_sb.append(vt_in)
+            x_sb.append(xt_in)
+
+        def transpose_pair(src, bank):
+            for a in range(2):
+                words = src[:, a, :].bitcast(F32)
+                for u in range(2):
+                    nc.tensor.transpose(
+                        bank[:, u * 256 + a * P : u * 256 + (a + 1) * P],
+                        words[:, u * P : (u + 1) * P],
+                        ident[:],
+                    )
+
+        def words_out(bank):
+            return bank[:].rearrange("p (u m) -> p m u", u=2)
+
+        def halves_out(bank):
+            return bank[:].bitcast(BF16).rearrange("p (u m e) -> p m u e", u=2, e=2)
+
+        pv_t = ps_v.tile([P, 512], F32, name="pv_t", tag="vt")
+        transpose_pair(pv_sb, pv_t)
+        pm_t = ps_x.tile([P, 512], F32, name="pm_t", tag="xt")
+        transpose_pair(pm_sb, pm_t)
+        gp = const.tile([P, 2, 1024], BF16, name="gp", align_bytes=64)
+        nc.scalar.activation(
+            out=gp[:, 1, :].rearrange("p (m u e) -> p m u e", u=2, e=2),
+            in_=halves_out(pv_t),
+            func=ACT.Sqrt,
+            scale=LAMDA * LAMDA * 4.0,
+        )
+        nc.vector.tensor_scalar(
+            out=gp[:, 0, :].rearrange("p (m u e) -> p m u e", u=2, e=2),
+            in0=halves_out(pm_t),
+            scalar1=2.0,
+            scalar2=None,
+            op0=ALU.mult,
+        )
+        p_codes = const.tile([P, 512], U32, name="p_codes", align_bytes=64)
+        p_scl = const.tile([P, 512], U8, name="p_scl", align_bytes=64)
+        nc.vector.quantize_mx(
+            out=p_codes[:].bitcast(FP8X4),
+            scales=p_scl[:],
+            in_=gp[:].rearrange("p s c -> p (s c)"),
+        )
+        spv = const.tile([P, 2], F32, name="spv")
+        for h in range(2):
+            junk = jpool.tile([P, D], BF16, name="junk")
+            nc.vector.tensor_scalar(
+                out=junk[:],
+                in0=pv_sb[:, h, :],
+                scalar1=-LAMDA,
+                scalar2=-2.0,
+                op0=ALU.mult,
+                op1=ALU.add,
+                accum_out=spv[:, h : h + 1],
+            )
+        rep = const.tile([P, 2, P], F32, name="rep")
+        for h in range(2):
+            nc.vector.tensor_copy(out=rep[:, h, :], in_=spv[:, h : h + 1].to_broadcast([P, P]))
+        sp_t = ps_o.tile([P, 512], F32, name="sp_t", tag="o")
+        for h in range(2):
+            nc.tensor.transpose(sp_t[:, h * P : (h + 1) * P], rep[:, h, :], ident[:])
+        spb = const.tile([P, J], F32, name="spb")
+        nc.vector.tensor_copy(out=spb[:], in_=sp_t[:, 0:J])
+
+        bias = const.tile([P, TILES], F32, name="bias")
+
+        banks = {}
+        grouped = {}
+        quant = {}
+        acc = {}
+
+        def stage_t(i):
+            vt = ps_v.tile([P, 512], F32, name="vt", tag="vt")
+            transpose_pair(v_sb[i], vt)
+            xt = ps_x.tile([P, 512], F32, name="xt", tag="xt")
+            transpose_pair(x_sb[i], xt)
+            banks[i] = (xt, vt)
+
+        def stage_ab(i):
+            xt, vt = banks[i]
+            g = gpool.tile([P, 2, 1024], BF16, name="g", align_bytes=64)
+            nc.scalar.activation(
+                out=g[:, 1, :].rearrange("p (m u e) -> p m u e", u=2, e=2),
+                in_=halves_out(vt),
+                func=ACT.Sqrt,
+            )
+            nc.scalar.copy(
+                out=g[:, 0, :].bitcast(F32).rearrange("p (m u) -> p m u", u=2),
+                in_=words_out(xt),
+            )
+            grouped[i] = g
+
+        def stage_c(i):
+            for a in range(2):
+                t = 2 * i + a
+                junk = jpool.tile([P, D], BF16, name="junk")
+                nc.vector.tensor_scalar(
+                    out=junk[:],
+                    in0=v_sb[i][:, a, :],
+                    scalar1=-LAMDA,
+                    scalar2=None,
+                    op0=ALU.mult,
+                    op1=ALU.add,
+                    accum_out=bias[:, t : t + 1],
+                )
+
+        def stage_q(i):
+            codes = qpool.tile([P, 512], U32, name="codes", align_bytes=64)
+            scl = qpool.tile([P, 512], U8, name="scl", align_bytes=64)
+            nc.vector.quantize_mx(
+                out=codes[:].bitcast(FP8X4),
+                scales=scl[:],
+                in_=grouped[i][:].rearrange("p s c -> p (s c)"),
+            )
+            quant[i] = (codes, scl)
+
+        def stage_m(i):
+            codes, scl = quant[i]
+            o = ps_o.tile([P, 512], F32, name="o", tag="o")
+            for a in range(2):
+                for s in range(2):
+                    lo = s * 256 + a * P
+                    nc.tensor.matmul_mx(
+                        out=o[:, a * J : (a + 1) * J],
+                        lhsT=codes[:, lo : lo + P].bitcast(FP8X4),
+                        lhsT_scale=scl[:, lo : lo + P],
+                        rhs=p_codes[:, s * J : (s + 1) * J].bitcast(FP8X4),
+                        rhs_scale=p_scl[:, s * J : (s + 1) * J],
+                        start=(s == 0),
+                        stop=(s == 1),
+                    )
+            acc[i] = o
+
+        def stage_e(i):
+            o = acc[i]
+            res = opool.tile([P, 2, J], F32, name="res")
+            for a in range(2):
+                t = 2 * i + a
+                nc.vector.scalar_tensor_tensor(
+                    out=res[:, a, :],
+                    in0=o[:, a * J : (a + 1) * J],
+                    scalar=bias[:, t : t + 1],
+                    in1=spb[:],
+                    op0=ALU.add,
+                    op1=ALU.add,
+                )
+            nc.sync.dma_start(out=o_v[:, 2 * i : 2 * i + 2, :], in_=res[:])
+
+        stage_t(0)
+        stage_t(1)
+        stage_c(0)
+        for i in range(PAIRS):
+            stage_ab(i)
+            if i + 2 < PAIRS:
+                stage_t(i + 2)
+            stage_q(i)
+            stage_m(i)
+            if i >= 1:
+                stage_e(i - 1)
+            if i + 1 < PAIRS:
+                stage_c(i + 1)
+        stage_e(PAIRS - 1)

@@ -7,6 +7,7 @@ FP8X4 = mybir.dt.float8_e4m3fn_x4
 BF16 = mybir.dt.bfloat16
 F32 = mybir.dt.float32
 U32 = mybir.dt.uint32
+I32 = mybir.dt.int32
 U8 = mybir.dt.uint8
 ALU = mybir.AluOpType
 ACT = mybir.ActivationFunctionType
@@ -20,6 +21,12 @@ TILES = N_ROWS // P
 PAIRS = TILES // 2
 
 FLOPS = 2 * 2 * N_ROWS * D * J
+
+WARM = 3
+HEAD_D = 1
+PAIR_D = 1
+SCALAR_SUMS = (7, 15, 23)
+SUMS_AHEAD = 2
 
 
 def tile_probprotoseghead_kernel(tc, x, x_var, proto_mean, proto_var, out):
@@ -38,8 +45,29 @@ def tile_probprotoseghead_kernel(tc, x, x_var, proto_mean, proto_var, out):
         opool = ctx.enter_context(tc.tile_pool(name="opool", bufs=4))
         jpool = ctx.enter_context(tc.tile_pool(name="jpool", bufs=2))
         ps_x = ctx.enter_context(tc.psum_pool(name="ps_x", bufs=2))
-        ps_v = ctx.enter_context(tc.psum_pool(name="ps_v", bufs=3))
+        ps_v = ctx.enter_context(tc.psum_pool(name="ps_v", bufs=2))
         ps_o = ctx.enter_context(tc.psum_pool(name="ps_o", bufs=3))
+        ps_d = ctx.enter_context(tc.psum_pool(name="ps_d", bufs=1))
+        ctx.enter_context(tc.manual_schedule())
+
+        z_codes = const.tile([P, 512], U32, name="z_codes", align_bytes=64)
+        z_scl = const.tile([P, 512], U8, name="z_scl", align_bytes=64)
+        z_in = const.tile([P, 2048], BF16, name="z_in", align_bytes=64)
+        nc.vector.memset(z_in[:].bitcast(I32), 0)
+        nc.vector.quantize_mx(out=z_codes[:].bitcast(FP8X4), scales=z_scl[:], in_=z_in[:])
+        d_bank = ps_d.tile([P, 512], F32, name="d_bank")
+
+        def dummy(count):
+            for w in range(count):
+                nc.tensor.matmul_mx(
+                    out=d_bank[:],
+                    lhsT=z_codes[:, 0:P].bitcast(FP8X4),
+                    lhsT_scale=z_scl[:, 0:P],
+                    rhs=z_codes[:].bitcast(FP8X4),
+                    rhs_scale=z_scl[:],
+                    start=True,
+                    stop=True,
+                )
 
         ident = const.tile([P, P], F32, name="ident")
         make_identity(nc, ident[:])
@@ -74,64 +102,26 @@ def tile_probprotoseghead_kernel(tc, x, x_var, proto_mean, proto_var, out):
         def halves_out(bank):
             return bank[:].bitcast(BF16).rearrange("p (u m e) -> p m u e", u=2, e=2)
 
-        pv_t = ps_v.tile([P, 512], F32, name="pv_t", tag="vt")
-        transpose_pair(pv_sb, pv_t)
-        pm_t = ps_x.tile([P, 512], F32, name="pm_t", tag="xt")
-        transpose_pair(pm_sb, pm_t)
-        gp = const.tile([P, 2, 1024], BF16, name="gp", align_bytes=64)
-        nc.scalar.activation(
-            out=gp[:, 1, :].rearrange("p (m u e) -> p m u e", u=2, e=2),
-            in_=halves_out(pv_t),
-            func=ACT.Sqrt,
-            scale=LAMDA * LAMDA * 4.0,
-        )
-        nc.vector.tensor_scalar(
-            out=gp[:, 0, :].rearrange("p (m u e) -> p m u e", u=2, e=2),
-            in0=halves_out(pm_t),
-            scalar1=2.0,
-            scalar2=None,
-            op0=ALU.mult,
-        )
-        p_codes = const.tile([P, 512], U32, name="p_codes", align_bytes=64)
-        p_scl = const.tile([P, 512], U8, name="p_scl", align_bytes=64)
-        nc.vector.quantize_mx(
-            out=p_codes[:].bitcast(FP8X4),
-            scales=p_scl[:],
-            in_=gp[:].rearrange("p s c -> p (s c)"),
-        )
-        spv = const.tile([P, 2], F32, name="spv")
-        for h in range(2):
-            junk = jpool.tile([P, D], BF16, name="junk")
-            nc.vector.tensor_scalar(
-                out=junk[:],
-                in0=pv_sb[:, h, :],
-                scalar1=-LAMDA,
-                scalar2=-2.0,
-                op0=ALU.mult,
-                op1=ALU.add,
-                accum_out=spv[:, h : h + 1],
-            )
-        rep = const.tile([P, 2, P], F32, name="rep")
-        for h in range(2):
-            nc.vector.tensor_copy(out=rep[:, h, :], in_=spv[:, h : h + 1].to_broadcast([P, P]))
-        sp_t = ps_o.tile([P, 512], F32, name="sp_t", tag="o")
-        for h in range(2):
-            nc.tensor.transpose(sp_t[:, h * P : (h + 1) * P], rep[:, h, :], ident[:])
-        spb = const.tile([P, J], F32, name="spb")
-        nc.vector.tensor_copy(out=spb[:], in_=sp_t[:, 0:J])
-
-        bias = const.tile([P, TILES], F32, name="bias")
+        bias_v = const.tile([P, TILES], F32, name="bias_v")
+        bias_s = const.tile([P, TILES], F32, name="bias_s")
 
         banks = {}
         grouped = {}
         quant = {}
         acc = {}
 
-        def stage_t(i):
+        def bias_of(t):
+            if t in SCALAR_SUMS:
+                return bias_s[:, t : t + 1]
+            return bias_v[:, t : t + 1]
+
+        def stage_t(i, head):
             vt = ps_v.tile([P, 512], F32, name="vt", tag="vt")
             transpose_pair(v_sb[i], vt)
+            dummy(head)
             xt = ps_x.tile([P, 512], F32, name="xt", tag="xt")
             transpose_pair(x_sb[i], xt)
+            dummy(head)
             banks[i] = (xt, vt)
 
         def stage_ab(i):
@@ -151,16 +141,26 @@ def tile_probprotoseghead_kernel(tc, x, x_var, proto_mean, proto_var, out):
         def stage_c(i):
             for a in range(2):
                 t = 2 * i + a
-                junk = jpool.tile([P, D], BF16, name="junk")
-                nc.vector.tensor_scalar(
-                    out=junk[:],
-                    in0=v_sb[i][:, a, :],
-                    scalar1=-LAMDA,
-                    scalar2=None,
-                    op0=ALU.mult,
-                    op1=ALU.add,
-                    accum_out=bias[:, t : t + 1],
-                )
+                if t in SCALAR_SUMS:
+                    junk_s = jpool.tile([P, D], BF16, name="junk_s")
+                    nc.scalar.activation(
+                        out=junk_s[:],
+                        in_=v_sb[i][:, a, :],
+                        func=ACT.Copy,
+                        scale=-LAMDA,
+                        accum_out=bias_of(t),
+                    )
+                else:
+                    junk = jpool.tile([P, D], BF16, name="junk")
+                    nc.vector.tensor_scalar(
+                        out=junk[:],
+                        in0=v_sb[i][:, a, :],
+                        scalar1=-LAMDA,
+                        scalar2=None,
+                        op0=ALU.mult,
+                        op1=ALU.add,
+                        accum_out=bias_of(t),
+                    )
 
         def stage_q(i):
             codes = qpool.tile([P, 512], U32, name="codes", align_bytes=64)
@@ -187,6 +187,7 @@ def tile_probprotoseghead_kernel(tc, x, x_var, proto_mean, proto_var, out):
                         start=(s == 0),
                         stop=(s == 1),
                     )
+            dummy(PAIR_D)
             acc[i] = o
 
         def stage_e(i):
@@ -197,24 +198,75 @@ def tile_probprotoseghead_kernel(tc, x, x_var, proto_mean, proto_var, out):
                 nc.vector.scalar_tensor_tensor(
                     out=res[:, a, :],
                     in0=o[:, a * J : (a + 1) * J],
-                    scalar=bias[:, t : t + 1],
+                    scalar=bias_of(t),
                     in1=spb[:],
                     op0=ALU.add,
                     op1=ALU.add,
                 )
             nc.sync.dma_start(out=o_v[:, 2 * i : 2 * i + 2, :], in_=res[:])
 
-        stage_t(0)
-        stage_t(1)
+        dummy(WARM)
+        pv_t = ps_v.tile([P, 512], F32, name="pv_t", tag="vt")
+        transpose_pair(pv_sb, pv_t)
+        dummy(HEAD_D)
+        pm_t = ps_x.tile([P, 512], F32, name="pm_t", tag="xt")
+        transpose_pair(pm_sb, pm_t)
+        dummy(HEAD_D)
+        gp = const.tile([P, 2, 1024], BF16, name="gp", align_bytes=64)
+        nc.scalar.activation(
+            out=gp[:, 1, :].rearrange("p (m u e) -> p m u e", u=2, e=2),
+            in_=halves_out(pv_t),
+            func=ACT.Sqrt,
+            scale=LAMDA * LAMDA * 4.0,
+        )
+        spv = const.tile([P, 2], F32, name="spv")
+        for h in range(2):
+            junk = jpool.tile([P, D], BF16, name="junk")
+            nc.vector.tensor_scalar(
+                out=junk[:],
+                in0=pv_sb[:, h, :],
+                scalar1=-LAMDA,
+                scalar2=-2.0,
+                op0=ALU.mult,
+                op1=ALU.add,
+                accum_out=spv[:, h : h + 1],
+            )
+        rep = const.tile([P, 2, P], F32, name="rep")
+        for h in range(2):
+            nc.vector.tensor_copy(out=rep[:, h, :], in_=spv[:, h : h + 1].to_broadcast([P, P]))
+        nc.vector.tensor_scalar(
+            out=gp[:, 0, :].rearrange("p (m u e) -> p m u e", u=2, e=2),
+            in0=halves_out(pm_t),
+            scalar1=2.0,
+            scalar2=None,
+            op0=ALU.mult,
+        )
+        stage_t(0, HEAD_D)
+        sp_t = ps_o.tile([P, 512], F32, name="sp_t", tag="o")
+        for h in range(2):
+            nc.tensor.transpose(sp_t[:, h * P : (h + 1) * P], rep[:, h, :], ident[:])
         stage_c(0)
+        p_codes = const.tile([P, 512], U32, name="p_codes", align_bytes=64)
+        p_scl = const.tile([P, 512], U8, name="p_scl", align_bytes=64)
+        nc.vector.quantize_mx(
+            out=p_codes[:].bitcast(FP8X4),
+            scales=p_scl[:],
+            in_=gp[:].rearrange("p s c -> p (s c)"),
+        )
+        spb = const.tile([P, J], F32, name="spb")
+        nc.vector.tensor_copy(out=spb[:], in_=sp_t[:, 0:J])
+        stage_t(1, HEAD_D)
+        for i in range(1, SUMS_AHEAD):
+            stage_c(i)
+
         for i in range(PAIRS):
             stage_ab(i)
             if i + 2 < PAIRS:
-                stage_t(i + 2)
+                stage_t(i + 2, 0)
             stage_q(i)
             stage_m(i)
             if i >= 1:
                 stage_e(i - 1)
-            if i + 1 < PAIRS:
-                stage_c(i + 1)
+            if i + SUMS_AHEAD < PAIRS:
+                stage_c(i + SUMS_AHEAD)
         stage_e(PAIRS - 1)

@@ -24,7 +24,7 @@ FLOPS = 2 * 2 * N_ROWS * D * J
 
 WARM = 3
 HEAD_D = 1
-PAIR_D = 1
+PAIR_D = 0
 SCALAR_SUMS = (7, 15, 23)
 SUMS_AHEAD = 2
 

@@ -7,7 +7,6 @@ FP8X4 = mybir.dt.float8_e4m3fn_x4
 BF16 = mybir.dt.bfloat16
 F32 = mybir.dt.float32
 U32 = mybir.dt.uint32
-I32 = mybir.dt.int32
 U8 = mybir.dt.uint8
 ALU = mybir.AluOpType
 ACT = mybir.ActivationFunctionType
@@ -19,13 +18,12 @@ J = 256
 LAMDA = 0.00390625
 TILES = N_ROWS // P
 PAIRS = TILES // 2
+LAST = PAIRS - 1
 
 FLOPS = 2 * 2 * N_ROWS * D * J
 
-WARM = 3
-HEAD_D = 1
-PAIR_D = 0
-SCALAR_SUMS = (7, 15, 23)
+SCALAR_SUMS = (0, 1, 13)
+VECTOR_COPIES = (0,)
 SUMS_AHEAD = 2
 
 
@@ -45,46 +43,27 @@ def tile_probprotoseghead_kernel(tc, x, x_var, proto_mean, proto_var, out):
         opool = ctx.enter_context(tc.tile_pool(name="opool", bufs=4))
         jpool = ctx.enter_context(tc.tile_pool(name="jpool", bufs=2))
         ps_x = ctx.enter_context(tc.psum_pool(name="ps_x", bufs=2))
-        ps_v = ctx.enter_context(tc.psum_pool(name="ps_v", bufs=2))
+        ps_v = ctx.enter_context(tc.psum_pool(name="ps_v", bufs=3))
         ps_o = ctx.enter_context(tc.psum_pool(name="ps_o", bufs=3))
-        ps_d = ctx.enter_context(tc.psum_pool(name="ps_d", bufs=1))
         ctx.enter_context(tc.manual_schedule())
-
-        z_codes = const.tile([P, 512], U32, name="z_codes", align_bytes=64)
-        z_scl = const.tile([P, 512], U8, name="z_scl", align_bytes=64)
-        z_in = const.tile([P, 2048], BF16, name="z_in", align_bytes=64)
-        nc.vector.memset(z_in[:].bitcast(I32), 0)
-        nc.vector.quantize_mx(out=z_codes[:].bitcast(FP8X4), scales=z_scl[:], in_=z_in[:])
-        d_bank = ps_d.tile([P, 512], F32, name="d_bank")
-
-        def dummy(count):
-            for w in range(count):
-                nc.tensor.matmul_mx(
-                    out=d_bank[:],
-                    lhsT=z_codes[:, 0:P].bitcast(FP8X4),
-                    lhsT_scale=z_scl[:, 0:P],
-                    rhs=z_codes[:].bitcast(FP8X4),
-                    rhs_scale=z_scl[:],
-                    start=True,
-                    stop=True,
-                )
 
         ident = const.tile([P, P], F32, name="ident")
         make_identity(nc, ident[:])
 
-        pv_sb = const.tile([P, 2, D], BF16, name="pv_sb")
-        nc.sync.dma_start(out=pv_sb[:], in_=pv_v)
-        pm_sb = const.tile([P, 2, D], BF16, name="pm_sb")
-        nc.sync.dma_start(out=pm_sb[:], in_=pm_v)
         x_sb = []
         v_sb = []
         for i in range(PAIRS):
-            vt_in = inp.tile([P, 2, D], BF16, name="v%d" % i)
-            nc.sync.dma_start(out=vt_in[:], in_=v_v[:, 2 * i : 2 * i + 2, :])
-            xt_in = inp.tile([P, 2, D], BF16, name="x%d" % i)
-            nc.sync.dma_start(out=xt_in[:], in_=x_v[:, 2 * i : 2 * i + 2, :])
-            v_sb.append(vt_in)
-            x_sb.append(xt_in)
+            v_sb.append(inp.tile([P, 2, D], BF16, name="v%d" % i))
+            x_sb.append(inp.tile([P, 2, D], BF16, name="x%d" % i))
+        pv_sb = const.tile([P, 2, D], BF16, name="pv_sb")
+        pm_sb = const.tile([P, 2, D], BF16, name="pm_sb")
+        nc.sync.dma_start(out=v_sb[0][:], in_=v_v[:, 0:2, :])
+        nc.sync.dma_start(out=pv_sb[:], in_=pv_v)
+        nc.sync.dma_start(out=pm_sb[:], in_=pm_v)
+        nc.sync.dma_start(out=x_sb[0][:], in_=x_v[:, 0:2, :])
+        for i in range(1, PAIRS):
+            nc.sync.dma_start(out=v_sb[i][:], in_=v_v[:, 2 * i : 2 * i + 2, :])
+            nc.sync.dma_start(out=x_sb[i][:], in_=x_v[:, 2 * i : 2 * i + 2, :])
 
         def transpose_pair(src, bank):
             for a in range(2):
@@ -102,10 +81,14 @@ def tile_probprotoseghead_kernel(tc, x, x_var, proto_mean, proto_var, out):
         def halves_out(bank):
             return bank[:].bitcast(BF16).rearrange("p (u m e) -> p m u e", u=2, e=2)
 
+        def halves_in(flat):
+            return flat.rearrange("p (m u e) -> p m u e", u=2, e=2)
+
         bias_v = const.tile([P, TILES], F32, name="bias_v")
         bias_s = const.tile([P, TILES], F32, name="bias_s")
 
-        banks = {}
+        x_bank = {}
+        v_bank = {}
         grouped = {}
         quant = {}
         acc = {}
@@ -115,110 +98,128 @@ def tile_probprotoseghead_kernel(tc, x, x_var, proto_mean, proto_var, out):
                 return bias_s[:, t : t + 1]
             return bias_v[:, t : t + 1]
 
-        def stage_t(i, head):
-            vt = ps_v.tile([P, 512], F32, name="vt", tag="vt")
-            transpose_pair(v_sb[i], vt)
-            dummy(head)
-            xt = ps_x.tile([P, 512], F32, name="xt", tag="xt")
-            transpose_pair(x_sb[i], xt)
-            dummy(head)
-            banks[i] = (xt, vt)
+        def stage_tv(i):
+            v_bank[i] = ps_v.tile([P, 512], F32, name="vt", tag="vt")
+            transpose_pair(v_sb[i], v_bank[i])
 
-        def stage_ab(i):
-            xt, vt = banks[i]
-            g = gpool.tile([P, 2, 1024], BF16, name="g", align_bytes=64)
+        def stage_tx(i):
+            x_bank[i] = ps_x.tile([P, 512], F32, name="xt", tag="xt")
+            transpose_pair(x_sb[i], x_bank[i])
+
+        def stage_g(i):
+            grouped[i] = gpool.tile([P, 2, 1024], BF16, name="g", align_bytes=64)
+
+        def stage_b(i):
             nc.scalar.activation(
-                out=g[:, 1, :].rearrange("p (m u e) -> p m u e", u=2, e=2),
-                in_=halves_out(vt),
+                out=halves_in(grouped[i][:, 1, :]), in_=halves_out(v_bank[i]), func=ACT.Sqrt
+            )
+
+        def stage_b_half(i, a):
+            nc.scalar.activation(
+                out=halves_in(grouped[i][:, 1, a * D : (a + 1) * D]),
+                in_=halves_out(v_bank[i])[:, a * P : (a + 1) * P, :, :],
                 func=ACT.Sqrt,
             )
-            nc.scalar.copy(
-                out=g[:, 0, :].bitcast(F32).rearrange("p (m u) -> p m u", u=2),
-                in_=words_out(xt),
-            )
-            grouped[i] = g
+
+        def stage_a(i):
+            dst = grouped[i][:, 0, :].bitcast(F32).rearrange("p (m u) -> p m u", u=2)
+            if i in VECTOR_COPIES:
+                nc.vector.tensor_copy(out=dst, in_=words_out(x_bank[i]))
+            else:
+                nc.scalar.copy(out=dst, in_=words_out(x_bank[i]))
+
+        def stage_c1(t):
+            src = v_sb[t // 2][:, t % 2, :]
+            if t in SCALAR_SUMS:
+                junk_s = jpool.tile([P, D], BF16, name="junk_s")
+                nc.scalar.activation(
+                    out=junk_s[:], in_=src, func=ACT.Copy, scale=-LAMDA, accum_out=bias_of(t)
+                )
+            else:
+                junk = jpool.tile([P, D], BF16, name="junk")
+                nc.vector.tensor_scalar(
+                    out=junk[:],
+                    in0=src,
+                    scalar1=-LAMDA,
+                    scalar2=None,
+                    op0=ALU.mult,
+                    op1=ALU.add,
+                    accum_out=bias_of(t),
+                )
 
         def stage_c(i):
-            for a in range(2):
-                t = 2 * i + a
-                if t in SCALAR_SUMS:
-                    junk_s = jpool.tile([P, D], BF16, name="junk_s")
-                    nc.scalar.activation(
-                        out=junk_s[:],
-                        in_=v_sb[i][:, a, :],
-                        func=ACT.Copy,
-                        scale=-LAMDA,
-                        accum_out=bias_of(t),
-                    )
-                else:
-                    junk = jpool.tile([P, D], BF16, name="junk")
-                    nc.vector.tensor_scalar(
-                        out=junk[:],
-                        in0=v_sb[i][:, a, :],
-                        scalar1=-LAMDA,
-                        scalar2=None,
-                        op0=ALU.mult,
-                        op1=ALU.add,
-                        accum_out=bias_of(t),
-                    )
+            stage_c1(2 * i)
+            stage_c1(2 * i + 1)
 
-        def stage_q(i):
+        def stage_qt(i):
             codes = qpool.tile([P, 512], U32, name="codes", align_bytes=64)
             scl = qpool.tile([P, 512], U8, name="scl", align_bytes=64)
-            nc.vector.quantize_mx(
-                out=codes[:].bitcast(FP8X4),
-                scales=scl[:],
-                in_=grouped[i][:].rearrange("p s c -> p (s c)"),
-            )
             quant[i] = (codes, scl)
 
-        def stage_m(i):
+        def stage_q(i, lo, width):
             codes, scl = quant[i]
+            nc.vector.quantize_mx(
+                out=codes[:, lo // 4 : (lo + width) // 4].bitcast(FP8X4),
+                scales=scl[:, lo // 4 : (lo + width) // 4],
+                in_=grouped[i][:].rearrange("p s c -> p (s c)")[:, lo : lo + width],
+            )
+
+        def passes(i, a, dst):
+            codes, scl = quant[i]
+            for s in range(2):
+                lo = s * 256 + a * P
+                nc.tensor.matmul_mx(
+                    out=dst,
+                    lhsT=codes[:, lo : lo + P].bitcast(FP8X4),
+                    lhsT_scale=scl[:, lo : lo + P],
+                    rhs=p_codes[:, s * J : (s + 1) * J].bitcast(FP8X4),
+                    rhs_scale=p_scl[:, s * J : (s + 1) * J],
+                    start=(s == 0),
+                    stop=(s == 1),
+                )
+
+        def stage_m(i):
             o = ps_o.tile([P, 512], F32, name="o", tag="o")
             for a in range(2):
-                for s in range(2):
-                    lo = s * 256 + a * P
-                    nc.tensor.matmul_mx(
-                        out=o[:, a * J : (a + 1) * J],
-                        lhsT=codes[:, lo : lo + P].bitcast(FP8X4),
-                        lhsT_scale=scl[:, lo : lo + P],
-                        rhs=p_codes[:, s * J : (s + 1) * J].bitcast(FP8X4),
-                        rhs_scale=p_scl[:, s * J : (s + 1) * J],
-                        start=(s == 0),
-                        stop=(s == 1),
-                    )
-            dummy(PAIR_D)
-            acc[i] = o
+                passes(i, a, o[:, a * J : (a + 1) * J])
+                acc[2 * i + a] = o[:, a * J : (a + 1) * J]
+
+        def stage_m_half(i, a):
+            o = ps_o.tile([P, 512], F32, name="o", tag="o")
+            passes(i, a, o[:, 0:J])
+            acc[2 * i + a] = o[:, 0:J]
+
+        def combine(t, dst):
+            nc.vector.scalar_tensor_tensor(
+                out=dst, in0=acc[t], scalar=bias_of(t), in1=spb[:], op0=ALU.add, op1=ALU.add
+            )
 
         def stage_e(i):
-            o = acc[i]
             res = opool.tile([P, 2, J], F32, name="res")
             for a in range(2):
-                t = 2 * i + a
-                nc.vector.scalar_tensor_tensor(
-                    out=res[:, a, :],
-                    in0=o[:, a * J : (a + 1) * J],
-                    scalar=bias_of(t),
-                    in1=spb[:],
-                    op0=ALU.add,
-                    op1=ALU.add,
-                )
+                combine(2 * i + a, res[:, a, :])
             nc.sync.dma_start(out=o_v[:, 2 * i : 2 * i + 2, :], in_=res[:])
 
-        dummy(WARM)
+        def stage_e_half(t):
+            res1 = opool.tile([P, 1, J], F32, name="res1")
+            combine(t, res1[:, 0, :])
+            nc.sync.dma_start(out=o_v[:, t : t + 1, :], in_=res1[:])
+
+        stage_tv(0)
         pv_t = ps_v.tile([P, 512], F32, name="pv_t", tag="vt")
         transpose_pair(pv_sb, pv_t)
-        dummy(HEAD_D)
         pm_t = ps_x.tile([P, 512], F32, name="pm_t", tag="xt")
         transpose_pair(pm_sb, pm_t)
-        dummy(HEAD_D)
+        stage_tx(0)
+
+        stage_c(0)
+        stage_g(0)
+        stage_b(0)
         gp = const.tile([P, 2, 1024], BF16, name="gp", align_bytes=64)
         nc.scalar.activation(
-            out=gp[:, 1, :].rearrange("p (m u e) -> p m u e", u=2, e=2),
-            in_=halves_out(pv_t),
-            func=ACT.Sqrt,
-            scale=LAMDA * LAMDA * 4.0,
+            out=halves_in(gp[:, 1, :]), in_=halves_out(pv_t), func=ACT.Sqrt, scale=LAMDA * LAMDA * 4.0
         )
+
         spv = const.tile([P, 2], F32, name="spv")
         for h in range(2):
             junk = jpool.tile([P, D], BF16, name="junk")
@@ -234,39 +235,49 @@ def tile_probprotoseghead_kernel(tc, x, x_var, proto_mean, proto_var, out):
         rep = const.tile([P, 2, P], F32, name="rep")
         for h in range(2):
             nc.vector.tensor_copy(out=rep[:, h, :], in_=spv[:, h : h + 1].to_broadcast([P, P]))
-        nc.vector.tensor_scalar(
-            out=gp[:, 0, :].rearrange("p (m u e) -> p m u e", u=2, e=2),
-            in0=halves_out(pm_t),
-            scalar1=2.0,
-            scalar2=None,
-            op0=ALU.mult,
-        )
-        stage_t(0, HEAD_D)
         sp_t = ps_o.tile([P, 512], F32, name="sp_t", tag="o")
         for h in range(2):
             nc.tensor.transpose(sp_t[:, h * P : (h + 1) * P], rep[:, h, :], ident[:])
-        stage_c(0)
+        nc.vector.tensor_scalar(
+            out=halves_in(gp[:, 0, :]), in0=halves_out(pm_t), scalar1=2.0, scalar2=None, op0=ALU.mult
+        )
+        stage_tv(1)
+        stage_tx(1)
+        stage_c(1)
+        stage_a(0)
         p_codes = const.tile([P, 512], U32, name="p_codes", align_bytes=64)
         p_scl = const.tile([P, 512], U8, name="p_scl", align_bytes=64)
         nc.vector.quantize_mx(
-            out=p_codes[:].bitcast(FP8X4),
-            scales=p_scl[:],
-            in_=gp[:].rearrange("p s c -> p (s c)"),
+            out=p_codes[:].bitcast(FP8X4), scales=p_scl[:], in_=gp[:].rearrange("p s c -> p (s c)")
         )
         spb = const.tile([P, J], F32, name="spb")
         nc.vector.tensor_copy(out=spb[:], in_=sp_t[:, 0:J])
-        stage_t(1, HEAD_D)
-        for i in range(1, SUMS_AHEAD):
-            stage_c(i)
 
-        for i in range(PAIRS):
-            stage_ab(i)
+        for i in range(LAST):
+            if i >= 1:
+                stage_g(i)
+                stage_b(i)
+                stage_a(i)
             if i + 2 < PAIRS:
-                stage_t(i + 2, 0)
-            stage_q(i)
+                stage_tv(i + 2)
+                stage_tx(i + 2)
+            stage_qt(i)
+            stage_q(i, 0, 2048)
             stage_m(i)
             if i >= 1:
                 stage_e(i - 1)
             if i + SUMS_AHEAD < PAIRS:
                 stage_c(i + SUMS_AHEAD)
-        stage_e(PAIRS - 1)
+
+        stage_g(LAST)
+        stage_a(LAST)
+        stage_b_half(LAST, 0)
+        stage_b_half(LAST, 1)
+        stage_qt(LAST)
+        stage_q(LAST, 0, 1024)
+        stage_e(LAST - 1)
+        for a in range(2):
+            stage_q(LAST, 1024 + a * D, D)
+            stage_m_half(LAST, a)
+        for a in range(2):
+            stage_e_half(2 * LAST + a)

@@ -24,6 +24,9 @@ FLOPS = 2 * 2 * N_ROWS * D * J
 
 SCALAR_SUMS = (0, 1, 13)
 VECTOR_COPIES = (0,)
+WARM = 5
+HEAD_PAIRS = 3
+HEAD_W = 256
 SUMS_AHEAD = 2
 
 
@@ -43,9 +46,24 @@ def tile_probprotoseghead_kernel(tc, x, x_var, proto_mean, proto_var, out):
         opool = ctx.enter_context(tc.tile_pool(name="opool", bufs=4))
         jpool = ctx.enter_context(tc.tile_pool(name="jpool", bufs=2))
         ps_x = ctx.enter_context(tc.psum_pool(name="ps_x", bufs=2))
-        ps_v = ctx.enter_context(tc.psum_pool(name="ps_v", bufs=3))
+        ps_v = ctx.enter_context(tc.psum_pool(name="ps_v", bufs=2))
         ps_o = ctx.enter_context(tc.psum_pool(name="ps_o", bufs=3))
+        ps_d = ctx.enter_context(tc.psum_pool(name="ps_d", bufs=1))
         ctx.enter_context(tc.manual_schedule())
+
+        zeros = const.tile([P, 512], BF16, name="zeros")
+        nc.vector.memset(zeros[:], 0.0)
+        d_bank = ps_d.tile([P, 512], F32, name="d_bank")
+
+        def dummy(count, width):
+            for w in range(count):
+                nc.tensor.matmul(
+                    out=d_bank[:, 0:width],
+                    lhsT=zeros[:, 0:P],
+                    rhs=zeros[:, 0:width],
+                    start=True,
+                    stop=True,
+                )
 
         ident = const.tile([P, P], F32, name="ident")
         make_identity(nc, ident[:])
@@ -101,10 +119,14 @@ def tile_probprotoseghead_kernel(tc, x, x_var, proto_mean, proto_var, out):
         def stage_tv(i):
             v_bank[i] = ps_v.tile([P, 512], F32, name="vt", tag="vt")
             transpose_pair(v_sb[i], v_bank[i])
+            if i < HEAD_PAIRS:
+                dummy(1, HEAD_W)
 
         def stage_tx(i):
             x_bank[i] = ps_x.tile([P, 512], F32, name="xt", tag="xt")
             transpose_pair(x_sb[i], x_bank[i])
+            if i < HEAD_PAIRS:
+                dummy(1, HEAD_W)
 
         def stage_g(i):
             grouped[i] = gpool.tile([P, 2, 1024], BF16, name="g", align_bytes=64)
@@ -205,11 +227,14 @@ def tile_probprotoseghead_kernel(tc, x, x_var, proto_mean, proto_var, out):
             combine(t, res1[:, 0, :])
             nc.sync.dma_start(out=o_v[:, t : t + 1, :], in_=res1[:])
 
+        dummy(WARM, 512)
         stage_tv(0)
         pv_t = ps_v.tile([P, 512], F32, name="pv_t", tag="vt")
         transpose_pair(pv_sb, pv_t)
+        dummy(1, HEAD_W)
         pm_t = ps_x.tile([P, 512], F32, name="pm_t", tag="xt")
         transpose_pair(pm_sb, pm_t)
+        dummy(1, HEAD_W)
         stage_tx(0)
 
         stage_c(0)

@@ -24,9 +24,6 @@ FLOPS = 2 * 2 * N_ROWS * D * J
 
 SCALAR_SUMS = (0, 1, 13)
 VECTOR_COPIES = (0,)
-WARM = 5
-HEAD_PAIRS = 3
-HEAD_W = 256
 SUMS_AHEAD = 2
 
 
@@ -41,29 +38,19 @@ def tile_probprotoseghead_kernel(tc, x, x_var, proto_mean, proto_var, out):
     with ExitStack() as ctx:
         const = ctx.enter_context(tc.tile_pool(name="const", bufs=1))
         inp = ctx.enter_context(tc.tile_pool(name="inp", bufs=1))
-        gpool = ctx.enter_context(tc.tile_pool(name="gpool", bufs=3))
-        qpool = ctx.enter_context(tc.tile_pool(name="qpool", bufs=4))
-        opool = ctx.enter_context(tc.tile_pool(name="opool", bufs=4))
+        gpool = ctx.enter_context(tc.tile_pool(name="gpool", bufs=4))
+        qpool = ctx.enter_context(tc.tile_pool(name="qpool", bufs=6))
+        opool = ctx.enter_context(tc.tile_pool(name="opool", bufs=PAIRS))
         jpool = ctx.enter_context(tc.tile_pool(name="jpool", bufs=2))
         ps_x = ctx.enter_context(tc.psum_pool(name="ps_x", bufs=2))
-        ps_v = ctx.enter_context(tc.psum_pool(name="ps_v", bufs=2))
+        ps_v = ctx.enter_context(tc.psum_pool(name="ps_v", bufs=3))
         ps_o = ctx.enter_context(tc.psum_pool(name="ps_o", bufs=3))
-        ps_d = ctx.enter_context(tc.psum_pool(name="ps_d", bufs=1))
         ctx.enter_context(tc.manual_schedule())
 
-        zeros = const.tile([P, 512], BF16, name="zeros")
-        nc.vector.memset(zeros[:], 0.0)
-        d_bank = ps_d.tile([P, 512], F32, name="d_bank")
-
-        def dummy(count, width):
-            for w in range(count):
-                nc.tensor.matmul(
-                    out=d_bank[:, 0:width],
-                    lhsT=zeros[:, 0:P],
-                    rhs=zeros[:, 0:width],
-                    start=True,
-                    stop=True,
-                )
+        one = const.tile([P, 1], F32, name="one")
+        nc.vector.memset(one[:], 1.0)
+        one_root = const.tile([P, 1], F32, name="one_root")
+        nc.scalar.activation(out=one_root[:], in_=one[:], func=ACT.Sqrt)
 
         ident = const.tile([P, P], F32, name="ident")
         make_identity(nc, ident[:])
@@ -119,14 +106,10 @@ def tile_probprotoseghead_kernel(tc, x, x_var, proto_mean, proto_var, out):
         def stage_tv(i):
             v_bank[i] = ps_v.tile([P, 512], F32, name="vt", tag="vt")
             transpose_pair(v_sb[i], v_bank[i])
-            if i < HEAD_PAIRS:
-                dummy(1, HEAD_W)
 
         def stage_tx(i):
             x_bank[i] = ps_x.tile([P, 512], F32, name="xt", tag="xt")
             transpose_pair(x_sb[i], x_bank[i])
-            if i < HEAD_PAIRS:
-                dummy(1, HEAD_W)
 
         def stage_g(i):
             grouped[i] = gpool.tile([P, 2, 1024], BF16, name="g", align_bytes=64)
@@ -227,14 +210,11 @@ def tile_probprotoseghead_kernel(tc, x, x_var, proto_mean, proto_var, out):
             combine(t, res1[:, 0, :])
             nc.sync.dma_start(out=o_v[:, t : t + 1, :], in_=res1[:])
 
-        dummy(WARM, 512)
         stage_tv(0)
         pv_t = ps_v.tile([P, 512], F32, name="pv_t", tag="vt")
         transpose_pair(pv_sb, pv_t)
-        dummy(1, HEAD_W)
         pm_t = ps_x.tile([P, 512], F32, name="pm_t", tag="xt")
         transpose_pair(pm_sb, pm_t)
-        dummy(1, HEAD_W)
         stage_tx(0)
 
         stage_c(0)

@@ -22,9 +22,11 @@ LAST = PAIRS - 1
 
 FLOPS = 2 * 2 * N_ROWS * D * J
 
-SCALAR_SUMS = (0, 1, 13)
-VECTOR_COPIES = (0,)
+SCALAR_SUMS = (0, 13)
 SUMS_AHEAD = 2
+WARM = 5
+HEAD_GROUPS = 8
+HEAD_W = 256
 
 
 def tile_probprotoseghead_kernel(tc, x, x_var, proto_mean, proto_var, out):
@@ -43,8 +45,9 @@ def tile_probprotoseghead_kernel(tc, x, x_var, proto_mean, proto_var, out):
         opool = ctx.enter_context(tc.tile_pool(name="opool", bufs=PAIRS))
         jpool = ctx.enter_context(tc.tile_pool(name="jpool", bufs=2))
         ps_x = ctx.enter_context(tc.psum_pool(name="ps_x", bufs=2))
-        ps_v = ctx.enter_context(tc.psum_pool(name="ps_v", bufs=3))
+        ps_v = ctx.enter_context(tc.psum_pool(name="ps_v", bufs=2))
         ps_o = ctx.enter_context(tc.psum_pool(name="ps_o", bufs=3))
+        ps_d = ctx.enter_context(tc.psum_pool(name="ps_d", bufs=1))
         ctx.enter_context(tc.manual_schedule())
 
         one = const.tile([P, 1], F32, name="one")
@@ -52,33 +55,54 @@ def tile_probprotoseghead_kernel(tc, x, x_var, proto_mean, proto_var, out):
         one_root = const.tile([P, 1], F32, name="one_root")
         nc.scalar.activation(out=one_root[:], in_=one[:], func=ACT.Sqrt)
 
+        zeros = const.tile([P, 512], BF16, name="zeros")
+        nc.vector.memset(zeros[:], 0.0)
+        d_bank = ps_d.tile([P, 512], F32, name="d_bank")
+        groups_done = []
+
+        def dummy(width):
+            nc.tensor.matmul(
+                out=d_bank[:, 0:width], lhsT=zeros[:, 0:P], rhs=zeros[:, 0:width], start=True, stop=True
+            )
+
         ident = const.tile([P, P], F32, name="ident")
         make_identity(nc, ident[:])
 
-        x_sb = []
-        v_sb = []
-        for i in range(PAIRS):
-            v_sb.append(inp.tile([P, 2, D], BF16, name="v%d" % i))
-            x_sb.append(inp.tile([P, 2, D], BF16, name="x%d" % i))
+        x_rows = []
+        v_rows = []
+        v0a = inp.tile([P, D], BF16, name="v0a")
+        v0b = inp.tile([P, D], BF16, name="v0b")
+        nc.sync.dma_start(out=v0a[:], in_=v_v[:, 0, :])
+        nc.sync.dma_start(out=v0b[:], in_=v_v[:, 1, :])
+        v_rows.append(v0a[:])
+        v_rows.append(v0b[:])
         pv_sb = const.tile([P, 2, D], BF16, name="pv_sb")
         pm_sb = const.tile([P, 2, D], BF16, name="pm_sb")
-        nc.sync.dma_start(out=v_sb[0][:], in_=v_v[:, 0:2, :])
         nc.sync.dma_start(out=pv_sb[:], in_=pv_v)
         nc.sync.dma_start(out=pm_sb[:], in_=pm_v)
-        nc.sync.dma_start(out=x_sb[0][:], in_=x_v[:, 0:2, :])
-        for i in range(1, PAIRS):
-            nc.sync.dma_start(out=v_sb[i][:], in_=v_v[:, 2 * i : 2 * i + 2, :])
-            nc.sync.dma_start(out=x_sb[i][:], in_=x_v[:, 2 * i : 2 * i + 2, :])
+        for i in range(PAIRS):
+            if i >= 1:
+                v_in = inp.tile([P, 2, D], BF16, name="v%d" % i)
+                nc.sync.dma_start(out=v_in[:], in_=v_v[:, 2 * i : 2 * i + 2, :])
+                v_rows.append(v_in[:, 0, :])
+                v_rows.append(v_in[:, 1, :])
+            x_in = inp.tile([P, 2, D], BF16, name="x%d" % i)
+            nc.sync.dma_start(out=x_in[:], in_=x_v[:, 2 * i : 2 * i + 2, :])
+            x_rows.append(x_in[:, 0, :])
+            x_rows.append(x_in[:, 1, :])
 
-        def transpose_pair(src, bank):
-            for a in range(2):
-                words = src[:, a, :].bitcast(F32)
+        def transpose_pair(rows_a, rows_b, bank):
+            for a, rows in enumerate((rows_a, rows_b)):
+                words = rows.bitcast(F32)
                 for u in range(2):
                     nc.tensor.transpose(
                         bank[:, u * 256 + a * P : u * 256 + (a + 1) * P],
                         words[:, u * P : (u + 1) * P],
                         ident[:],
                     )
+            groups_done.append(1)
+            if len(groups_done) <= HEAD_GROUPS:
+                dummy(HEAD_W)
 
         def words_out(bank):
             return bank[:].rearrange("p (u m) -> p m u", u=2)
@@ -105,46 +129,35 @@ def tile_probprotoseghead_kernel(tc, x, x_var, proto_mean, proto_var, out):
 
         def stage_tv(i):
             v_bank[i] = ps_v.tile([P, 512], F32, name="vt", tag="vt")
-            transpose_pair(v_sb[i], v_bank[i])
+            transpose_pair(v_rows[2 * i], v_rows[2 * i + 1], v_bank[i])
 
         def stage_tx(i):
             x_bank[i] = ps_x.tile([P, 512], F32, name="xt", tag="xt")
-            transpose_pair(x_sb[i], x_bank[i])
-
-        def stage_g(i):
-            grouped[i] = gpool.tile([P, 2, 1024], BF16, name="g", align_bytes=64)
+            transpose_pair(x_rows[2 * i], x_rows[2 * i + 1], x_bank[i])
 
         def stage_b(i):
+            grouped[i] = gpool.tile([P, 2, 1024], BF16, name="g", align_bytes=64)
             nc.scalar.activation(
                 out=halves_in(grouped[i][:, 1, :]), in_=halves_out(v_bank[i]), func=ACT.Sqrt
             )
 
-        def stage_b_half(i, a):
-            nc.scalar.activation(
-                out=halves_in(grouped[i][:, 1, a * D : (a + 1) * D]),
-                in_=halves_out(v_bank[i])[:, a * P : (a + 1) * P, :, :],
-                func=ACT.Sqrt,
+        def stage_a(i):
+            nc.scalar.copy(
+                out=grouped[i][:, 0, :].bitcast(F32).rearrange("p (m u) -> p m u", u=2),
+                in_=words_out(x_bank[i]),
             )
 
-        def stage_a(i):
-            dst = grouped[i][:, 0, :].bitcast(F32).rearrange("p (m u) -> p m u", u=2)
-            if i in VECTOR_COPIES:
-                nc.vector.tensor_copy(out=dst, in_=words_out(x_bank[i]))
-            else:
-                nc.scalar.copy(out=dst, in_=words_out(x_bank[i]))
-
-        def stage_c1(t):
-            src = v_sb[t // 2][:, t % 2, :]
+        def stage_c(t):
             if t in SCALAR_SUMS:
                 junk_s = jpool.tile([P, D], BF16, name="junk_s")
                 nc.scalar.activation(
-                    out=junk_s[:], in_=src, func=ACT.Copy, scale=-LAMDA, accum_out=bias_of(t)
+                    out=junk_s[:], in_=v_rows[t], func=ACT.Copy, scale=-LAMDA, accum_out=bias_of(t)
                 )
             else:
                 junk = jpool.tile([P, D], BF16, name="junk")
                 nc.vector.tensor_scalar(
                     out=junk[:],
-                    in0=src,
+                    in0=v_rows[t],
                     scalar1=-LAMDA,
                     scalar2=None,
                     op0=ALU.mult,
@@ -152,78 +165,67 @@ def tile_probprotoseghead_kernel(tc, x, x_var, proto_mean, proto_var, out):
                     accum_out=bias_of(t),
                 )
 
-        def stage_c(i):
-            stage_c1(2 * i)
-            stage_c1(2 * i + 1)
-
-        def stage_qt(i):
+        def stage_q(i):
             codes = qpool.tile([P, 512], U32, name="codes", align_bytes=64)
             scl = qpool.tile([P, 512], U8, name="scl", align_bytes=64)
+            nc.vector.quantize_mx(
+                out=codes[:].bitcast(FP8X4),
+                scales=scl[:],
+                in_=grouped[i][:].rearrange("p s c -> p (s c)"),
+            )
             quant[i] = (codes, scl)
 
-        def stage_q(i, lo, width):
-            codes, scl = quant[i]
-            nc.vector.quantize_mx(
-                out=codes[:, lo // 4 : (lo + width) // 4].bitcast(FP8X4),
-                scales=scl[:, lo // 4 : (lo + width) // 4],
-                in_=grouped[i][:].rearrange("p s c -> p (s c)")[:, lo : lo + width],
-            )
-
-        def passes(i, a, dst):
-            codes, scl = quant[i]
-            for s in range(2):
-                lo = s * 256 + a * P
-                nc.tensor.matmul_mx(
-                    out=dst,
-                    lhsT=codes[:, lo : lo + P].bitcast(FP8X4),
-                    lhsT_scale=scl[:, lo : lo + P],
-                    rhs=p_codes[:, s * J : (s + 1) * J].bitcast(FP8X4),
-                    rhs_scale=p_scl[:, s * J : (s + 1) * J],
-                    start=(s == 0),
-                    stop=(s == 1),
-                )
-
         def stage_m(i):
+            codes, scl = quant[i]
             o = ps_o.tile([P, 512], F32, name="o", tag="o")
             for a in range(2):
-                passes(i, a, o[:, a * J : (a + 1) * J])
-                acc[2 * i + a] = o[:, a * J : (a + 1) * J]
+                for s in range(2):
+                    lo = s * 256 + a * P
+                    nc.tensor.matmul_mx(
+                        out=o[:, a * J : (a + 1) * J],
+                        lhsT=codes[:, lo : lo + P].bitcast(FP8X4),
+                        lhsT_scale=scl[:, lo : lo + P],
+                        rhs=p_codes[:, s * J : (s + 1) * J].bitcast(FP8X4),
+                        rhs_scale=p_scl[:, s * J : (s + 1) * J],
+                        start=(s == 0),
+                        stop=(s == 1),
+                    )
+            acc[i] = o
 
-        def stage_m_half(i, a):
-            o = ps_o.tile([P, 512], F32, name="o", tag="o")
-            passes(i, a, o[:, 0:J])
-            acc[2 * i + a] = o[:, 0:J]
-
-        def combine(t, dst):
-            nc.vector.scalar_tensor_tensor(
-                out=dst, in0=acc[t], scalar=bias_of(t), in1=spb[:], op0=ALU.add, op1=ALU.add
-            )
-
-        def stage_e(i):
+        def stage_e(i, stores):
             res = opool.tile([P, 2, J], F32, name="res")
             for a in range(2):
-                combine(2 * i + a, res[:, a, :])
-            nc.sync.dma_start(out=o_v[:, 2 * i : 2 * i + 2, :], in_=res[:])
+                t = 2 * i + a
+                nc.vector.scalar_tensor_tensor(
+                    out=res[:, a, :],
+                    in0=acc[i][:, a * J : (a + 1) * J],
+                    scalar=bias_of(t),
+                    in1=spb[:],
+                    op0=ALU.add,
+                    op1=ALU.add,
+                )
+                if stores == 2:
+                    nc.sync.dma_start(out=o_v[:, t : t + 1, :], in_=res[:, a : a + 1, :])
+            if stores == 1:
+                nc.sync.dma_start(out=o_v[:, 2 * i : 2 * i + 2, :], in_=res[:])
 
-        def stage_e_half(t):
-            res1 = opool.tile([P, 1, J], F32, name="res1")
-            combine(t, res1[:, 0, :])
-            nc.sync.dma_start(out=o_v[:, t : t + 1, :], in_=res1[:])
-
+        for w in range(WARM):
+            dummy(512)
         stage_tv(0)
         pv_t = ps_v.tile([P, 512], F32, name="pv_t", tag="vt")
-        transpose_pair(pv_sb, pv_t)
+        transpose_pair(pv_sb[:, 0, :], pv_sb[:, 1, :], pv_t)
         pm_t = ps_x.tile([P, 512], F32, name="pm_t", tag="xt")
-        transpose_pair(pm_sb, pm_t)
+        transpose_pair(pm_sb[:, 0, :], pm_sb[:, 1, :], pm_t)
         stage_tx(0)
 
         stage_c(0)
-        stage_g(0)
+        stage_c(1)
         stage_b(0)
         gp = const.tile([P, 2, 1024], BF16, name="gp", align_bytes=64)
         nc.scalar.activation(
             out=halves_in(gp[:, 1, :]), in_=halves_out(pv_t), func=ACT.Sqrt, scale=LAMDA * LAMDA * 4.0
         )
+        stage_a(0)
 
         spv = const.tile([P, 2], F32, name="spv")
         for h in range(2):
@@ -248,8 +250,8 @@ def tile_probprotoseghead_kernel(tc, x, x_var, proto_mean, proto_var, out):
         )
         stage_tv(1)
         stage_tx(1)
-        stage_c(1)
-        stage_a(0)
+        stage_c(2)
+        stage_c(3)
         p_codes = const.tile([P, 512], U32, name="p_codes", align_bytes=64)
         p_scl = const.tile([P, 512], U8, name="p_scl", align_bytes=64)
         nc.vector.quantize_mx(
@@ -258,31 +260,20 @@ def tile_probprotoseghead_kernel(tc, x, x_var, proto_mean, proto_var, out):
         spb = const.tile([P, J], F32, name="spb")
         nc.vector.tensor_copy(out=spb[:], in_=sp_t[:, 0:J])
 
-        for i in range(LAST):
+        for i in range(PAIRS):
             if i >= 1:
-                stage_g(i)
                 stage_b(i)
                 stage_a(i)
             if i + 2 < PAIRS:
                 stage_tv(i + 2)
                 stage_tx(i + 2)
-            stage_qt(i)
-            stage_q(i, 0, 2048)
+            stage_q(i)
             stage_m(i)
-            if i >= 1:
-                stage_e(i - 1)
+            if 1 <= i < LAST - 1:
+                stage_e(i - 1, 1)
             if i + SUMS_AHEAD < PAIRS:
-                stage_c(i + SUMS_AHEAD)
-
-        stage_g(LAST)
-        stage_a(LAST)
-        stage_b_half(LAST, 0)
-        stage_b_half(LAST, 1)
-        stage_qt(LAST)
-        stage_q(LAST, 0, 1024)
-        stage_e(LAST - 1)
-        for a in range(2):
-            stage_q(LAST, 1024 + a * D, D)
-            stage_m_half(LAST, a)
-        for a in range(2):
-            stage_e_half(2 * LAST + a)
+                stage_c(2 * (i + SUMS_AHEAD))
+                stage_c(2 * (i + SUMS_AHEAD) + 1)
+        stage_e(LAST - 2, 1)
+        stage_e(LAST - 1, 1)
+        stage_e(LAST, 2)

@@ -26,7 +26,7 @@ SCALAR_SUMS = (0, 13)
 SUMS_AHEAD = 2
 WARM = 5
 HEAD_GROUPS = 8
-HEAD_W = 256
+HEAD_W = 128
 
 
 def tile_probprotoseghead_kernel(tc, x, x_var, proto_mean, proto_var, out):
@@ -55,14 +55,14 @@ def tile_probprotoseghead_kernel(tc, x, x_var, proto_mean, proto_var, out):
         one_root = const.tile([P, 1], F32, name="one_root")
         nc.scalar.activation(out=one_root[:], in_=one[:], func=ACT.Sqrt)
 
-        zeros = const.tile([P, 512], BF16, name="zeros")
+        zeros = const.tile([P, P], F32, name="zeros")
         nc.vector.memset(zeros[:], 0.0)
         d_bank = ps_d.tile([P, 512], F32, name="d_bank")
         groups_done = []
 
         def dummy(width):
             nc.tensor.matmul(
-                out=d_bank[:, 0:width], lhsT=zeros[:, 0:P], rhs=zeros[:, 0:width], start=True, stop=True
+                out=d_bank[:, 0:width], lhsT=zeros[:], rhs=zeros[:, 0:width], start=True, stop=True
             )
 
         ident = const.tile([P, P], F32, name="ident")
@@ -210,7 +210,7 @@ def tile_probprotoseghead_kernel(tc, x, x_var, proto_mean, proto_var, out):
                 nc.sync.dma_start(out=o_v[:, 2 * i : 2 * i + 2, :], in_=res[:])
 
         for w in range(WARM):
-            dummy(512)
+            dummy(P)
         stage_tv(0)
         pv_t = ps_v.tile([P, 512], F32, name="pv_t", tag="vt")
         transpose_pair(pv_sb[:, 0, :], pv_sb[:, 1, :], pv_t)

@@ -22,11 +22,11 @@ LAST = PAIRS - 1
 
 FLOPS = 2 * 2 * N_ROWS * D * J
 
-SCALAR_SUMS = (0, 13)
-SUMS_AHEAD = 2
-WARM = 5
-HEAD_GROUPS = 8
-HEAD_W = 128
+FOLDED = (9, 11, 13, 15, 17, 19, 21, 23)
+SCALAR_SUMS = (0,)
+SUMS_AHEAD = 3
+WARM = 3
+FOLD_W = 64
 
 
 def tile_probprotoseghead_kernel(tc, x, x_var, proto_mean, proto_var, out):
@@ -46,7 +46,7 @@ def tile_probprotoseghead_kernel(tc, x, x_var, proto_mean, proto_var, out):
         jpool = ctx.enter_context(tc.tile_pool(name="jpool", bufs=2))
         ps_x = ctx.enter_context(tc.psum_pool(name="ps_x", bufs=2))
         ps_v = ctx.enter_context(tc.psum_pool(name="ps_v", bufs=2))
-        ps_o = ctx.enter_context(tc.psum_pool(name="ps_o", bufs=3))
+        ps_o = ctx.enter_context(tc.psum_pool(name="ps_o", bufs=2))
         ps_d = ctx.enter_context(tc.psum_pool(name="ps_d", bufs=1))
         ctx.enter_context(tc.manual_schedule())
 
@@ -57,16 +57,30 @@ def tile_probprotoseghead_kernel(tc, x, x_var, proto_mean, proto_var, out):
 
         zeros = const.tile([P, P], F32, name="zeros")
         nc.vector.memset(zeros[:], 0.0)
-        d_bank = ps_d.tile([P, 512], F32, name="d_bank")
-        groups_done = []
+        d_bank = ps_d.tile([P, 2, FOLD_W], F32, name="d_bank")
+        f_bank = ps_d.tile([P, 4, FOLD_W], F32, name="f_bank")
 
-        def dummy(width):
-            nc.tensor.matmul(
-                out=d_bank[:, 0:width], lhsT=zeros[:], rhs=zeros[:, 0:width], start=True, stop=True
-            )
+        def dummy():
+            nc.tensor.matmul(out=d_bank[:, 0:2, :], lhsT=zeros[:], rhs=zeros[:], start=True, stop=True)
 
         ident = const.tile([P, P], F32, name="ident")
         make_identity(nc, ident[:])
+        fold_by = const.tile([P, P], BF16, name="fold_by")
+        nc.vector.tensor_scalar(out=fold_by[:], in0=ident[:], scalar1=-LAMDA, scalar2=None, op0=ALU.mult)
+
+        def fold_out(slot):
+            return (d_bank if slot % 2 else f_bank)[:, 0, :]
+
+        def fold(rows, slot):
+            steps = D // FOLD_W
+            for c in range(steps):
+                nc.tensor.matmul(
+                    out=fold_out(slot),
+                    lhsT=fold_by[:],
+                    rhs=rows[:, c * FOLD_W : (c + 1) * FOLD_W],
+                    start=(c == 0),
+                    stop=(c == steps - 1),
+                )
 
         x_rows = []
         v_rows = []
@@ -78,8 +92,8 @@ def tile_probprotoseghead_kernel(tc, x, x_var, proto_mean, proto_var, out):
         v_rows.append(v0b[:])
         pv_sb = const.tile([P, 2, D], BF16, name="pv_sb")
         pm_sb = const.tile([P, 2, D], BF16, name="pm_sb")
-        nc.sync.dma_start(out=pv_sb[:], in_=pv_v)
         nc.sync.dma_start(out=pm_sb[:], in_=pm_v)
+        nc.sync.dma_start(out=pv_sb[:], in_=pv_v)
         for i in range(PAIRS):
             if i >= 1:
                 v_in = inp.tile([P, 2, D], BF16, name="v%d" % i)
@@ -100,9 +114,6 @@ def tile_probprotoseghead_kernel(tc, x, x_var, proto_mean, proto_var, out):
                         words[:, u * P : (u + 1) * P],
                         ident[:],
                     )
-            groups_done.append(1)
-            if len(groups_done) <= HEAD_GROUPS:
-                dummy(HEAD_W)
 
         def words_out(bank):
             return bank[:].rearrange("p (u m) -> p m u", u=2)
@@ -115,6 +126,7 @@ def tile_probprotoseghead_kernel(tc, x, x_var, proto_mean, proto_var, out):
 
         bias_v = const.tile([P, TILES], F32, name="bias_v")
         bias_s = const.tile([P, TILES], F32, name="bias_s")
+        bias_f = const.tile([P, 8], F32, name="bias_f")
 
         x_bank = {}
         v_bank = {}
@@ -125,6 +137,9 @@ def tile_probprotoseghead_kernel(tc, x, x_var, proto_mean, proto_var, out):
         def bias_of(t):
             if t in SCALAR_SUMS:
                 return bias_s[:, t : t + 1]
+            if t in FOLDED:
+                slot = FOLDED.index(t)
+                return bias_f[:, slot : slot + 1]
             return bias_v[:, t : t + 1]
 
         def stage_tv(i):
@@ -147,7 +162,14 @@ def tile_probprotoseghead_kernel(tc, x, x_var, proto_mean, proto_var, out):
                 in_=words_out(x_bank[i]),
             )
 
+        def fold_sum(slot):
+            nc.vector.tensor_reduce(
+                out=bias_f[:, slot : slot + 1], in_=fold_out(slot), axis=mybir.AxisListType.X, op=ALU.add
+            )
+
         def stage_c(t):
+            if t in FOLDED:
+                return
             if t in SCALAR_SUMS:
                 junk_s = jpool.tile([P, D], BF16, name="junk_s")
                 nc.scalar.activation(
@@ -210,25 +232,28 @@ def tile_probprotoseghead_kernel(tc, x, x_var, proto_mean, proto_var, out):
                 nc.sync.dma_start(out=o_v[:, 2 * i : 2 * i + 2, :], in_=res[:])
 
         for w in range(WARM):
-            dummy(P)
-        stage_tv(0)
-        pv_t = ps_v.tile([P, 512], F32, name="pv_t", tag="vt")
-        transpose_pair(pv_sb[:, 0, :], pv_sb[:, 1, :], pv_t)
-        pm_t = ps_x.tile([P, 512], F32, name="pm_t", tag="xt")
-        transpose_pair(pm_sb[:, 0, :], pm_sb[:, 1, :], pm_t)
-        stage_tx(0)
+            dummy()
+        pm2 = const.tile([P, 2, D], BF16, name="pm2")
+        gp = const.tile([P, 2, 1024], BF16, name="gp", align_bytes=64)
+        p_codes = const.tile([P, 512], U32, name="p_codes", align_bytes=64)
+        p_scl = const.tile([P, 512], U8, name="p_scl", align_bytes=64)
+        spb = const.tile([P, J], F32, name="spb")
 
         stage_c(0)
         stage_c(1)
+        stage_tv(0)
         stage_b(0)
-        gp = const.tile([P, 2, 1024], BF16, name="gp", align_bytes=64)
+        nc.vector.tensor_scalar(out=pm2[:], in0=pm_sb[:], scalar1=2.0, scalar2=None, op0=ALU.mult)
+        pm_t = ps_x.tile([P, 512], F32, name="pm_t", tag="xt")
+        transpose_pair(pm2[:, 0, :], pm2[:, 1, :], pm_t)
+        pv_t = ps_v.tile([P, 512], F32, name="pv_t", tag="vt")
+        transpose_pair(pv_sb[:, 0, :], pv_sb[:, 1, :], pv_t)
         nc.scalar.activation(
             out=halves_in(gp[:, 1, :]), in_=halves_out(pv_t), func=ACT.Sqrt, scale=LAMDA * LAMDA * 4.0
         )
-        stage_a(0)
-
         spv = const.tile([P, 2], F32, name="spv")
-        for h in range(2):
+
+        def proto_sum(h):
             junk = jpool.tile([P, D], BF16, name="junk")
             nc.vector.tensor_scalar(
                 out=junk[:],
@@ -239,41 +264,48 @@ def tile_probprotoseghead_kernel(tc, x, x_var, proto_mean, proto_var, out):
                 op1=ALU.add,
                 accum_out=spv[:, h : h + 1],
             )
-        rep = const.tile([P, 2, P], F32, name="rep")
-        for h in range(2):
-            nc.vector.tensor_copy(out=rep[:, h, :], in_=spv[:, h : h + 1].to_broadcast([P, P]))
+
+        proto_sum(0)
+        nc.vector.tensor_copy(out=gp[:, 0, :].bitcast(F32).rearrange("p (m u) -> p m u", u=2), in_=words_out(pm_t))
+        proto_sum(1)
+        stage_tx(0)
+        stage_a(0)
+        dummy()
+        stage_tv(1)
+        dummy()
+        stage_tx(1)
         sp_t = ps_o.tile([P, 512], F32, name="sp_t", tag="o")
         for h in range(2):
-            nc.tensor.transpose(sp_t[:, h * P : (h + 1) * P], rep[:, h, :], ident[:])
-        nc.vector.tensor_scalar(
-            out=halves_in(gp[:, 0, :]), in0=halves_out(pm_t), scalar1=2.0, scalar2=None, op0=ALU.mult
-        )
-        stage_tv(1)
-        stage_tx(1)
+            nc.tensor.transpose(sp_t[:, h * P : (h + 1) * P], spv[:, h : h + 1].to_broadcast([P, P]), ident[:])
+        dummy()
+        stage_tv(2)
         stage_c(2)
         stage_c(3)
-        p_codes = const.tile([P, 512], U32, name="p_codes", align_bytes=64)
-        p_scl = const.tile([P, 512], U8, name="p_scl", align_bytes=64)
         nc.vector.quantize_mx(
             out=p_codes[:].bitcast(FP8X4), scales=p_scl[:], in_=gp[:].rearrange("p s c -> p (s c)")
         )
-        spb = const.tile([P, J], F32, name="spb")
-        nc.vector.tensor_copy(out=spb[:], in_=sp_t[:, 0:J])
 
         for i in range(PAIRS):
-            if i >= 1:
-                stage_b(i)
-                stage_a(i)
             if i + 2 < PAIRS:
-                stage_tv(i + 2)
                 stage_tx(i + 2)
+            if i + 1 < PAIRS:
+                stage_b(i + 1)
+            if i + 3 < PAIRS:
+                stage_tv(i + 3)
+            if i + 1 < PAIRS:
+                stage_a(i + 1)
             stage_q(i)
+            if 2 <= i < 10:
+                fold(v_rows[FOLDED[i - 2]], i - 2)
             stage_m(i)
-            if 1 <= i < LAST - 1:
+            if i == 0:
+                nc.vector.tensor_copy(out=spb[:], in_=sp_t[:, 0:J])
+            if 3 <= i < 11:
+                fold_sum(i - 3)
+            if i + 2 < PAIRS:
+                stage_c(2 * (i + 2))
+                stage_c(2 * (i + 2) + 1)
+            if 1 <= i < LAST:
                 stage_e(i - 1, 1)
-            if i + SUMS_AHEAD < PAIRS:
-                stage_c(2 * (i + SUMS_AHEAD))
-                stage_c(2 * (i + SUMS_AHEAD) + 1)
-        stage_e(LAST - 2, 1)
         stage_e(LAST - 1, 1)
         stage_e(LAST, 2)

from contextlib import ExitStack

import concourse.mybir as mybir
from concourse.masks import make_identity

FP8X4 = mybir.dt.float8_e4m3fn_x4
BF16 = mybir.dt.bfloat16
F32 = mybir.dt.float32
U32 = mybir.dt.uint32
U8 = mybir.dt.uint8
ALU = mybir.AluOpType
ACT = mybir.ActivationFunctionType

P = 128
N_ROWS = 3072
D = 512
J = 256
LAMDA = 0.00390625
TILES = N_ROWS // P
PAIRS = TILES // 2
LAST = PAIRS - 1

FLOPS = 2 * 2 * N_ROWS * D * J

FOLDED = (9, 11, 13, 15, 17, 19, 21, 23)
SCALAR_SUMS = (0,)
SUMS_AHEAD = 3
WARM = 3
FOLD_W = 64


def tile_probprotoseghead_kernel(tc, x, x_var, proto_mean, proto_var, out):
    nc = tc.nc
    x_v = x.rearrange("(p t) d -> p t d", t=TILES)
    v_v = x_var.rearrange("(p t) d -> p t d", t=TILES)
    o_v = out.rearrange("(p t) c m -> p t (c m)", t=TILES)
    pm_v = proto_mean.rearrange("c m d -> (c m) d").rearrange("(h p) d -> p h d", p=P)
    pv_v = proto_var.rearrange("c m d -> (c m) d").rearrange("(h p) d -> p h d", p=P)

    with ExitStack() as ctx:
        const = ctx.enter_context(tc.tile_pool(name="const", bufs=1))
        inp = ctx.enter_context(tc.tile_pool(name="inp", bufs=1))
        gpool = ctx.enter_context(tc.tile_pool(name="gpool", bufs=4))
        qpool = ctx.enter_context(tc.tile_pool(name="qpool", bufs=6))
        opool = ctx.enter_context(tc.tile_pool(name="opool", bufs=PAIRS))
        jpool = ctx.enter_context(tc.tile_pool(name="jpool", bufs=2))
        ps_x = ctx.enter_context(tc.psum_pool(name="ps_x", bufs=2))
        ps_v = ctx.enter_context(tc.psum_pool(name="ps_v", bufs=2))
        ps_o = ctx.enter_context(tc.psum_pool(name="ps_o", bufs=2))
        ps_d = ctx.enter_context(tc.psum_pool(name="ps_d", bufs=1))
        ctx.enter_context(tc.manual_schedule())

        one = const.tile([P, 1], F32, name="one")
        nc.vector.memset(one[:], 1.0)
        one_root = const.tile([P, 1], F32, name="one_root")
        nc.scalar.activation(out=one_root[:], in_=one[:], func=ACT.Sqrt)

        zeros = const.tile([P, P], F32, name="zeros")
        nc.vector.memset(zeros[:], 0.0)
        d_bank = ps_d.tile([P, 2, FOLD_W], F32, name="d_bank")
        f_bank = ps_d.tile([P, 4, FOLD_W], F32, name="f_bank")

        def dummy():
            nc.tensor.matmul(out=d_bank[:, 0:2, :], lhsT=zeros[:], rhs=zeros[:], start=True, stop=True)

        ident = const.tile([P, P], F32, name="ident")
        make_identity(nc, ident[:])
        fold_by = const.tile([P, P], BF16, name="fold_by")
        nc.vector.tensor_scalar(out=fold_by[:], in0=ident[:], scalar1=-LAMDA, scalar2=None, op0=ALU.mult)

        def fold_out(slot):
            return (d_bank if slot % 2 else f_bank)[:, 0, :]

        def fold(rows, slot):
            steps = D // FOLD_W
            for c in range(steps):
                nc.tensor.matmul(
                    out=fold_out(slot),
                    lhsT=fold_by[:],
                    rhs=rows[:, c * FOLD_W : (c + 1) * FOLD_W],
                    start=(c == 0),
                    stop=(c == steps - 1),
                )

        x_rows = []
        v_rows = []
        v0a = inp.tile([P, D], BF16, name="v0a")
        v0b = inp.tile([P, D], BF16, name="v0b")
        nc.sync.dma_start(out=v0a[:], in_=v_v[:, 0, :])
        nc.sync.dma_start(out=v0b[:], in_=v_v[:, 1, :])
        v_rows.append(v0a[:])
        v_rows.append(v0b[:])
        pv_sb = const.tile([P, 2, D], BF16, name="pv_sb")
        pm_sb = const.tile([P, 2, D], BF16, name="pm_sb")
        nc.sync.dma_start(out=pm_sb[:], in_=pm_v)
        nc.sync.dma_start(out=pv_sb[:], in_=pv_v)
        for i in range(PAIRS):
            if i >= 1:
                v_in = inp.tile([P, 2, D], BF16, name="v%d" % i)
                nc.sync.dma_start(out=v_in[:], in_=v_v[:, 2 * i : 2 * i + 2, :])
                v_rows.append(v_in[:, 0, :])
                v_rows.append(v_in[:, 1, :])
            x_in = inp.tile([P, 2, D], BF16, name="x%d" % i)
            nc.sync.dma_start(out=x_in[:], in_=x_v[:, 2 * i : 2 * i + 2, :])
            x_rows.append(x_in[:, 0, :])
            x_rows.append(x_in[:, 1, :])

        def transpose_pair(rows_a, rows_b, bank):
            for a, rows in enumerate((rows_a, rows_b)):
                words = rows.bitcast(F32)
                for u in range(2):
                    nc.tensor.transpose(
                        bank[:, u * 256 + a * P : u * 256 + (a + 1) * P],
                        words[:, u * P : (u + 1) * P],
                        ident[:],
                    )

        def words_out(bank):
            return bank[:].rearrange("p (u m) -> p m u", u=2)

        def halves_out(bank):
            return bank[:].bitcast(BF16).rearrange("p (u m e) -> p m u e", u=2, e=2)

        def halves_in(flat):
            return flat.rearrange("p (m u e) -> p m u e", u=2, e=2)

        bias_v = const.tile([P, TILES], F32, name="bias_v")
        bias_s = const.tile([P, TILES], F32, name="bias_s")
        bias_f = const.tile([P, 8], F32, name="bias_f")

        x_bank = {}
        v_bank = {}
        grouped = {}
        quant = {}
        acc = {}

        def bias_of(t):
            if t in SCALAR_SUMS:
                return bias_s[:, t : t + 1]
            if t in FOLDED:
                slot = FOLDED.index(t)
                return bias_f[:, slot : slot + 1]
            return bias_v[:, t : t + 1]

        def stage_tv(i):
            v_bank[i] = ps_v.tile([P, 512], F32, name="vt", tag="vt")
            transpose_pair(v_rows[2 * i], v_rows[2 * i + 1], v_bank[i])

        def stage_tx(i):
            x_bank[i] = ps_x.tile([P, 512], F32, name="xt", tag="xt")
            transpose_pair(x_rows[2 * i], x_rows[2 * i + 1], x_bank[i])

        def stage_b(i):
            grouped[i] = gpool.tile([P, 2, 1024], BF16, name="g", align_bytes=64)
            nc.scalar.activation(
                out=halves_in(grouped[i][:, 1, :]), in_=halves_out(v_bank[i]), func=ACT.Sqrt
            )

        def stage_a(i):
            nc.scalar.copy(
                out=grouped[i][:, 0, :].bitcast(F32).rearrange("p (m u) -> p m u", u=2),
                in_=words_out(x_bank[i]),
            )

        def fold_sum(slot):
            nc.vector.tensor_reduce(
                out=bias_f[:, slot : slot + 1], in_=fold_out(slot), axis=mybir.AxisListType.X, op=ALU.add
            )

        def stage_c(t):
            if t in FOLDED:
                return
            if t in SCALAR_SUMS:
                junk_s = jpool.tile([P, D], BF16, name="junk_s")
                nc.scalar.activation(
                    out=junk_s[:], in_=v_rows[t], func=ACT.Copy, scale=-LAMDA, accum_out=bias_of(t)
                )
            else:
                junk = jpool.tile([P, D], BF16, name="junk")
                nc.vector.tensor_scalar(
                    out=junk[:],
                    in0=v_rows[t],
                    scalar1=-LAMDA,
                    scalar2=None,
                    op0=ALU.mult,
                    op1=ALU.add,
                    accum_out=bias_of(t),
                )

        def stage_q(i):
            codes = qpool.tile([P, 512], U32, name="codes", align_bytes=64)
            scl = qpool.tile([P, 512], U8, name="scl", align_bytes=64)
            nc.vector.quantize_mx(
                out=codes[:].bitcast(FP8X4),
                scales=scl[:],
                in_=grouped[i][:].rearrange("p s c -> p (s c)"),
            )
            quant[i] = (codes, scl)

        def stage_m(i):
            codes, scl = quant[i]
            o = ps_o.tile([P, 512], F32, name="o", tag="o")
            for a in range(2):
                for s in range(2):
                    lo = s * 256 + a * P
                    nc.tensor.matmul_mx(
                        out=o[:, a * J : (a + 1) * J],
                        lhsT=codes[:, lo : lo + P].bitcast(FP8X4),
                        lhsT_scale=scl[:, lo : lo + P],
                        rhs=p_codes[:, s * J : (s + 1) * J].bitcast(FP8X4),
                        rhs_scale=p_scl[:, s * J : (s + 1) * J],
                        start=(s == 0),
                        stop=(s == 1),
                    )
            acc[i] = o

        def stage_e(i, stores):
            res = opool.tile([P, 2, J], F32, name="res")
            for a in range(2):
                t = 2 * i + a
                nc.vector.scalar_tensor_tensor(
                    out=res[:, a, :],
                    in0=acc[i][:, a * J : (a + 1) * J],
                    scalar=bias_of(t),
                    in1=spb[:],
                    op0=ALU.add,
                    op1=ALU.add,
                )
                if stores == 2:
                    nc.sync.dma_start(out=o_v[:, t : t + 1, :], in_=res[:, a : a + 1, :])
            if stores == 1:
                nc.sync.dma_start(out=o_v[:, 2 * i : 2 * i + 2, :], in_=res[:])

        for w in range(WARM):
            dummy()
        pm2 = const.tile([P, 2, D], BF16, name="pm2")
        gp = const.tile([P, 2, 1024], BF16, name="gp", align_bytes=64)
        p_codes = const.tile([P, 512], U32, name="p_codes", align_bytes=64)
        p_scl = const.tile([P, 512], U8, name="p_scl", align_bytes=64)
        spb = const.tile([P, J], F32, name="spb")

        stage_c(0)
        stage_c(1)
        stage_tv(0)
        stage_b(0)
        nc.vector.tensor_scalar(out=pm2[:], in0=pm_sb[:], scalar1=2.0, scalar2=None, op0=ALU.mult)
        pm_t = ps_x.tile([P, 512], F32, name="pm_t", tag="xt")
        transpose_pair(pm2[:, 0, :], pm2[:, 1, :], pm_t)
        pv_t = ps_v.tile([P, 512], F32, name="pv_t", tag="vt")
        transpose_pair(pv_sb[:, 0, :], pv_sb[:, 1, :], pv_t)
        nc.scalar.activation(
            out=halves_in(gp[:, 1, :]), in_=halves_out(pv_t), func=ACT.Sqrt, scale=LAMDA * LAMDA * 4.0
        )
        spv = const.tile([P, 2], F32, name="spv")

        def proto_sum(h):
            junk = jpool.tile([P, D], BF16, name="junk")
            nc.vector.tensor_scalar(
                out=junk[:],
                in0=pv_sb[:, h, :],
                scalar1=-LAMDA,
                scalar2=-2.0,
                op0=ALU.mult,
                op1=ALU.add,
                accum_out=spv[:, h : h + 1],
            )

        proto_sum(0)
        nc.vector.tensor_copy(out=gp[:, 0, :].bitcast(F32).rearrange("p (m u) -> p m u", u=2), in_=words_out(pm_t))
        proto_sum(1)
        stage_tx(0)
        stage_a(0)
        dummy()
        stage_tv(1)
        dummy()
        stage_tx(1)
        sp_t = ps_o.tile([P, 512], F32, name="sp_t", tag="o")
        for h in range(2):
            nc.tensor.transpose(sp_t[:, h * P : (h + 1) * P], spv[:, h : h + 1].to_broadcast([P, P]), ident[:])
        dummy()
        stage_tv(2)
        stage_c(2)
        stage_c(3)
        nc.vector.quantize_mx(
            out=p_codes[:].bitcast(FP8X4), scales=p_scl[:], in_=gp[:].rearrange("p s c -> p (s c)")
        )

        for i in range(PAIRS):
            if i + 2 < PAIRS:
                stage_tx(i + 2)
            if i + 1 < PAIRS:
                stage_b(i + 1)
            if i + 3 < PAIRS:
                stage_tv(i + 3)
            if i + 1 < PAIRS:
                stage_a(i + 1)
            stage_q(i)
            if 2 <= i < 10:
                fold(v_rows[FOLDED[i - 2]], i - 2)
            stage_m(i)
            if i == 0:
                nc.vector.tensor_copy(out=spb[:], in_=sp_t[:, 0:J])
            if 3 <= i < 11:
                fold_sum(i - 3)
            if i + 2 < PAIRS:
                stage_c(2 * (i + 2))
                stage_c(2 * (i + 2) + 1)
            if 1 <= i < LAST:
                stage_e(i - 1, 1)
        stage_e(LAST - 1, 1)
        stage_e(LAST, 2)
